import numpy as np
import ml_dtypes


def mxq(x, axis, fmt="e4m3"):
    dtype, down = {"e4m3": (ml_dtypes.float8_e4m3fn, 7), "e5m2": (ml_dtypes.float8_e5m2, 14)}[fmt]
    v = np.moveaxis(np.asarray(x, np.float32).astype(ml_dtypes.bfloat16).astype(np.float64), axis, -1)
    blocks = v.reshape(v.shape[:-1] + (-1, 32))
    amax = np.abs(blocks).max(-1, keepdims=True)
    byte = np.maximum(np.where(amax > 0, np.frexp(amax)[1] - 1 + 127, 0) - down, 1)
    scale = np.exp2(byte - 127.0)
    codes = (blocks / scale).astype(np.float32).astype(dtype).astype(np.float64)
    return np.moveaxis((codes * scale).reshape(v.shape), -1, axis)


WIDE = False


def mx_kscale(k):
    if not WIDE:
        return np.ones(k)
    levels = np.array([20, -20, 10, -10, 0])
    a = np.random.permutation(np.resize(levels, k // 512 * 4)).reshape(k // 512, 4)
    idx = np.arange(k)
    return np.exp2(a[idx // 512, idx % 128 // 32])


BF16 = ml_dtypes.bfloat16


def bf(x):
    return np.asarray(x, np.float32).astype(BF16)


def f64(x):
    return np.asarray(x).astype(np.float64)


NS, NI, T = 512, 128, 4097
NA = NS + NI


def setup_inputs():
    u = mx_kscale(NS)
    A = np.random.standard_normal((NS, NS)) / np.sqrt(NA)
    B = np.random.standard_normal((NS, NI)) / np.sqrt(NA)
    x0 = np.random.standard_normal(NS) * 3.0
    V = np.random.standard_normal((T, NA))
    V[0, :NS] *= 3.0
    g = np.random.standard_normal((T, NS)) * np.exp2(np.random.randint(-12, 1, (T, 1))) * 4.0
    V[:, :NS] = V[:, :NS] / u[None, :]
    return {"A": bf(A * u[None, :] / u[:, None]), "B": bf(B / u[:, None]), "x0": bf(x0 / u),
            "net_input": bf(V.reshape(-1)), "T": T, "grad_out": bf((g * u[None, :]).reshape(-1))}


def reference(A, B, x0, net_input, T, grad_out):
    n_state = A.shape[0]
    n_all = n_state + B.shape[1]
    AB = np.concatenate([f64(A), f64(B)], axis=1)
    G = f64(grad_out).reshape(T, n_state)
    gV = np.zeros((T, n_all))
    gV[:-1] = mxq(G[1:], 1, "e5m2") @ mxq(AB, 0, "e4m3")
    gV[0, :n_state] += G[0]
    gV[1:, :n_state] -= G[1:]
    return gV.reshape(-1)

@@ -1,0 +1,163 @@
+from contextlib import ExitStack
+
+import concourse.mybir as mybir
+from concourse.masks import make_identity
+
+BF16 = mybir.dt.bfloat16
+F32 = mybir.dt.float32
+U32 = mybir.dt.uint32
+U8 = mybir.dt.uint8
+E5M2_X4 = mybir.dt.float8_e5m2_x4
+E4M3_X4 = mybir.dt.float8_e4m3fn_x4
+
+P = 128
+PACK = 4
+NS = 512
+NI = 128
+NA = NS + NI
+STEPS = 4096
+TILES = STEPS // P
+GROUP = 4
+N_GROUPS = TILES // GROUP
+WORDS = NS // 2
+N_PASS = 512
+
+FLOPS = 2 * STEPS * NS * NA
+BYTES = 2 * NS * NA + 2 * (STEPS + 1) * NS + 4 * (STEPS + 1) * NA
+
+
+def tile_constrainnet_t_kernel(tc, A, B, x0, net_input, T, grad_out, out):
+    nc = tc.nc
+    assert T == STEPS + 1
+
+    g_next = grad_out[NS : (STEPS + 1) * NS].rearrange("(p s k) -> p s k", p=P, k=NS)
+    g_first = grad_out[0 : STEPS * NS].rearrange("(p s k) -> p s k", p=P, k=NS)[:, 0, :]
+    g_last = grad_out[STEPS * NS : (STEPS + 1) * NS].rearrange("(o k) -> o k", o=1)
+    d_rows = out[0 : STEPS * NA].rearrange("(p j n) -> p j n", p=P, n=NA)
+    d_last = out[STEPS * NA : (STEPS + 1) * NA].rearrange("(o n) -> o n", o=1)
+
+    with ExitStack() as ctx:
+        ctx.enter_context(tc.manual_schedule())
+        keep = ctx.enter_context(tc.tile_pool(name="keep", bufs=1))
+        stage = ctx.enter_context(tc.tile_pool(name="stage", bufs=2))
+        psum_t = ctx.enter_context(tc.psum_pool(name="psum_t", bufs=2))
+        psum_a = ctx.enter_context(tc.psum_pool(name="psum_a", bufs=3))
+        psum_b = ctx.enter_context(tc.psum_pool(name="psum_b", bufs=3))
+
+        g_sb = keep.tile([P, (TILES + 1) * NS], BF16)
+        g_rows = g_sb[:].rearrange("p (s k) -> p s k", k=NS)
+        g_words = g_sb[:].bitcast(F32).rearrange("p (s w) -> p s w", w=WORDS)
+        g_codes = keep.tile([P, TILES * P], U32, align_bytes=64)
+        g_scales = keep.tile([P, TILES * P], U8, align_bytes=64)
+        a_raw = keep.tile([P, PACK, NS], BF16)
+        b_raw = keep.tile([P, PACK, NI], BF16)
+        ab_grouped = keep.tile([P, NA, PACK], BF16, align_bytes=64)
+        ab_codes = keep.tile([P, NA], U32, align_bytes=64)
+        ab_scales = keep.tile([P, NA], U8, align_bytes=64)
+        d_sb = keep.tile([P, TILES, NA], F32)
+        g_last_sb = keep.tile([1, NS], BF16)
+        d_last_sb = keep.tile([1, NA], F32)
+        identity = keep.tile([P, P], F32)
+
+        def load_weight(raw, weight):
+            for u in range(2):
+                nc.sync.dma_start(
+                    out=raw[:, 2 * u : 2 * u + 2, :],
+                    in_=weight[u * 2 * P : (u + 1) * 2 * P, :].rearrange("(q e) n -> q e n", e=2),
+                )
+
+        def load_group(c):
+            nc.sync.dma_start(
+                out=g_rows[:, 1 + c * GROUP : 1 + (c + 1) * GROUP, :],
+                in_=g_next[:, c * GROUP : (c + 1) * GROUP, :],
+            )
+
+        def regroup_weight(raw, cols):
+            nc.vector.tensor_copy(
+                out=ab_grouped[:, cols, :].rearrange("p (c i) t -> p c t i", i=4),
+                in_=raw[:].rearrange("p t (c i) -> p c t i", i=4),
+            )
+
+        def quantise_weight(cols):
+            nc.vector.quantize_mx(
+                out=ab_codes[:, cols].bitcast(E4M3_X4),
+                scales=ab_scales[:, cols],
+                in_=ab_grouped[:, cols, :].rearrange("p n t -> p (n t)"),
+            )
+
+        def transpose_group(c):
+            grouped = stage.tile([P, GROUP * P * PACK], BF16, align_bytes=64)
+            grouped_words = grouped[:].bitcast(F32).rearrange("p (j r u) -> p j r u", j=GROUP, u=2)
+            for half in range(GROUP // 2):
+                bank = psum_t.tile([P, 2, 2, P], F32)
+                for i in range(2):
+                    s = c * GROUP + 2 * half + i + 1
+                    for u in range(2):
+                        nc.tensor.transpose(
+                            bank[:, i, u, :], g_words[:, s, u * P : (u + 1) * P], identity[:]
+                        )
+                nc.scalar.copy(
+                    out=grouped_words[:, 2 * half : 2 * half + 2, :, :],
+                    in_=bank[:].rearrange("p i u r -> p i r u"),
+                )
+            return grouped
+
+        def quantise_group(c, grouped):
+            cols = slice(c * GROUP * P, (c + 1) * GROUP * P)
+            nc.vector.quantize_mx(
+                out=g_codes[:, cols].bitcast(E5M2_X4), scales=g_scales[:, cols], in_=grouped[:]
+            )
+
+        def multiply_tile(j):
+            cols = slice(j * P, (j + 1) * P)
+            acc_a = psum_a.tile([P, N_PASS], F32)
+            acc_b = psum_b.tile([P, N_PASS], F32)
+            for acc, first in ((acc_a, 0), (acc_b, NA - N_PASS)):
+                nc.tensor.matmul_mx(
+                    out=acc[:],
+                    lhsT=g_codes[:, cols].bitcast(E5M2_X4),
+                    lhsT_scale=g_scales[:, cols],
+                    rhs=ab_codes[:, first : first + N_PASS].bitcast(E4M3_X4),
+                    rhs_scale=ab_scales[:, first : first + N_PASS],
+                    start=True,
+                    stop=True,
+                )
+            nc.vector.tensor_tensor(
+                out=d_sb[:, j, 0:NS], in0=acc_a[:], in1=g_rows[:, j, :], op=mybir.AluOpType.subtract
+            )
+            nc.scalar.copy(out=d_sb[:, j, NS:NA], in_=acc_b[:, N_PASS - NI : N_PASS])
+
+        def store_group(c):
+            tiles = slice(c * GROUP, (c + 1) * GROUP)
+            nc.sync.dma_start(out=d_rows[:, tiles, :], in_=d_sb[:, tiles, :])
+
+        nc.sync.dma_start(out=g_last_sb[:], in_=g_last)
+        load_weight(a_raw, A)
+        load_group(0)
+        load_weight(b_raw, B)
+        nc.sync.dma_start(out=g_rows[:, 0, :], in_=g_first)
+        for c in range(1, N_GROUPS):
+            load_group(c)
+
+        make_identity(nc, identity[:])
+
+        nc.vector.memset(d_last_sb[:, NS:NA], 0.0)
+        nc.vector.tensor_scalar_mul(out=d_last_sb[:, 0:NS], in0=g_last_sb[:], scalar1=-1.0)
+        nc.sync.dma_start(out=d_last, in_=d_last_sb[:])
+
+        regroup_weight(a_raw, slice(0, NS))
+        regroup_weight(b_raw, slice(NS, NA))
+        quantise_weight(slice(0, NS))
+        quantise_weight(slice(NS, NA))
+
+        quantise_group(0, transpose_group(0))
+        nc.vector.tensor_scalar_mul(out=g_rows[0:1, 0, :], in0=g_rows[0:1, 0, :], scalar1=-1.0)
+        for c in range(N_GROUPS):
+            more = c + 1 < N_GROUPS
+            if more:
+                grouped_next = transpose_group(c + 1)
+            for i in range(GROUP):
+                if more and i == GROUP // 2:
+                    quantise_group(c + 1, grouped_next)
+                multiply_tile(c * GROUP + i)
+            store_group(c)

@@ -18,6 +18,7 @@ NA = NS + NI
 STEPS = 4096
 TILES = STEPS // P
 GROUP = 4
+STORE_TILES = 2
 N_GROUPS = TILES // GROUP
 WORDS = NS // 2
 N_PASS = 512
@@ -127,8 +128,7 @@ def tile_constrainnet_t_kernel(tc, A, B, x0, net_input, T, grad_out, out):
             )
             nc.scalar.copy(out=d_sb[:, j, NS:NA], in_=acc_b[:, N_PASS - NI : N_PASS])
 
-        def store_group(c):
-            tiles = slice(c * GROUP, (c + 1) * GROUP)
+        def store_tiles(tiles):
             nc.sync.dma_start(out=d_rows[:, tiles, :], in_=d_sb[:, tiles, :])
 
         nc.sync.dma_start(out=g_last_sb[:], in_=g_last)
@@ -159,5 +159,7 @@ def tile_constrainnet_t_kernel(tc, A, B, x0, net_input, T, grad_out, out):
             for i in range(GROUP):
                 if more and i == GROUP // 2:
                     quantise_group(c + 1, grouped_next)
-                multiply_tile(c * GROUP + i)
-            store_group(c)
+                j = c * GROUP + i
+                multiply_tile(j)
+                if (j + 1) % STORE_TILES == 0:
+                    store_tiles(slice(j + 1 - STORE_TILES, j + 1))

@@ -18,10 +18,9 @@ NA = NS + NI
 STEPS = 4096
 TILES = STEPS // P
 GROUP = 4
-STORE_TILES = 2
+HALF = GROUP // 2
 N_GROUPS = TILES // GROUP
 WORDS = NS // 2
-N_PASS = 512
 
 FLOPS = 2 * STEPS * NS * NA
 BYTES = 2 * NS * NA + 2 * (STEPS + 1) * NS + 4 * (STEPS + 1) * NA
@@ -40,10 +39,10 @@ def tile_constrainnet_t_kernel(tc, A, B, x0, net_input, T, grad_out, out):
     with ExitStack() as ctx:
         ctx.enter_context(tc.manual_schedule())
         keep = ctx.enter_context(tc.tile_pool(name="keep", bufs=1))
-        stage = ctx.enter_context(tc.tile_pool(name="stage", bufs=2))
+        stage = ctx.enter_context(tc.tile_pool(name="stage", bufs=3))
         psum_t = ctx.enter_context(tc.psum_pool(name="psum_t", bufs=2))
-        psum_a = ctx.enter_context(tc.psum_pool(name="psum_a", bufs=3))
-        psum_b = ctx.enter_context(tc.psum_pool(name="psum_b", bufs=3))
+        psum_a = ctx.enter_context(tc.psum_pool(name="psum_a", bufs=4))
+        psum_b = ctx.enter_context(tc.psum_pool(name="psum_b", bufs=1))
 
         g_sb = keep.tile([P, (TILES + 1) * NS], BF16)
         g_rows = g_sb[:].rearrange("p (s k) -> p s k", k=NS)
@@ -103,30 +102,52 @@ def tile_constrainnet_t_kernel(tc, A, B, x0, net_input, T, grad_out, out):
                 )
             return grouped
 
-        def quantise_group(c, grouped):
-            cols = slice(c * GROUP * P, (c + 1) * GROUP * P)
+        def quantise_half(c, half, grouped):
+            first = 2 * half * P
+            cols = slice(c * GROUP * P + first, c * GROUP * P + first + 2 * P)
             nc.vector.quantize_mx(
-                out=g_codes[:, cols].bitcast(E5M2_X4), scales=g_scales[:, cols], in_=grouped[:]
+                out=g_codes[:, cols].bitcast(E5M2_X4),
+                scales=g_scales[:, cols],
+                in_=grouped[:, first * PACK : (first + 2 * P) * PACK],
             )
 
-        def multiply_tile(j):
+        def multiply_by_a(j):
             cols = slice(j * P, (j + 1) * P)
-            acc_a = psum_a.tile([P, N_PASS], F32)
-            acc_b = psum_b.tile([P, N_PASS], F32)
-            for acc, first in ((acc_a, 0), (acc_b, NA - N_PASS)):
-                nc.tensor.matmul_mx(
-                    out=acc[:],
-                    lhsT=g_codes[:, cols].bitcast(E5M2_X4),
-                    lhsT_scale=g_scales[:, cols],
-                    rhs=ab_codes[:, first : first + N_PASS].bitcast(E4M3_X4),
-                    rhs_scale=ab_scales[:, first : first + N_PASS],
-                    start=True,
-                    stop=True,
-                )
-            nc.vector.tensor_tensor(
-                out=d_sb[:, j, 0:NS], in0=acc_a[:], in1=g_rows[:, j, :], op=mybir.AluOpType.subtract
+            acc = psum_a.tile([P, NS], F32)
+            nc.tensor.matmul_mx(
+                out=acc[:],
+                lhsT=g_codes[:, cols].bitcast(E5M2_X4),
+                lhsT_scale=g_scales[:, cols],
+                rhs=ab_codes[:, 0:NS].bitcast(E4M3_X4),
+                rhs_scale=ab_scales[:, 0:NS],
+                start=True,
+                stop=True,
             )
-            nc.scalar.copy(out=d_sb[:, j, NS:NA], in_=acc_b[:, N_PASS - NI : N_PASS])
+            nc.vector.tensor_tensor(
+                out=d_sb[:, j, 0:NS], in0=acc[:], in1=g_rows[:, j, :], op=mybir.AluOpType.subtract
+            )
+
+        def multiply_by_b(c):
+            cols = slice(c * GROUP * P, (c + 1) * GROUP * P)
+            acc_t = psum_b.tile([P, GROUP * P], F32)
+            nc.tensor.matmul_mx(
+                out=acc_t[:],
+                lhsT=ab_codes[:, NS:NA].bitcast(E4M3_X4),
+                lhsT_scale=ab_scales[:, NS:NA],
+                rhs=g_codes[:, cols].bitcast(E5M2_X4),
+                rhs_scale=g_scales[:, cols],
+                start=True,
+                stop=True,
+            )
+            product_t = stage.tile([P, GROUP * P], F32)
+            nc.scalar.copy(out=product_t[:], in_=acc_t[:])
+            return product_t
+
+        def transpose_back(c, product_t):
+            bank = psum_b.tile([P, GROUP, P], F32)
+            for i in range(GROUP):
+                nc.tensor.transpose(bank[:, i, :], product_t[:, i * P : (i + 1) * P], identity[:])
+            nc.scalar.copy(out=d_sb[:, c * GROUP : (c + 1) * GROUP, NS:NA], in_=bank[:])
 
         def store_tiles(tiles):
             nc.sync.dma_start(out=d_rows[:, tiles, :], in_=d_sb[:, tiles, :])
@@ -135,8 +156,9 @@ def tile_constrainnet_t_kernel(tc, A, B, x0, net_input, T, grad_out, out):
         load_weight(a_raw, A)
         load_group(0)
         load_weight(b_raw, B)
+        load_group(1)
         nc.sync.dma_start(out=g_rows[:, 0, :], in_=g_first)
-        for c in range(1, N_GROUPS):
+        for c in range(2, N_GROUPS):
             load_group(c)
 
         make_identity(nc, identity[:])
@@ -145,21 +167,26 @@ def tile_constrainnet_t_kernel(tc, A, B, x0, net_input, T, grad_out, out):
         nc.vector.tensor_scalar_mul(out=d_last_sb[:, 0:NS], in0=g_last_sb[:], scalar1=-1.0)
         nc.sync.dma_start(out=d_last, in_=d_last_sb[:])
 
-        regroup_weight(a_raw, slice(0, NS))
-        regroup_weight(b_raw, slice(NS, NA))
-        quantise_weight(slice(0, NS))
-        quantise_weight(slice(NS, NA))
+        for raw, cols in ((a_raw, slice(0, NS)), (b_raw, slice(NS, NA))):
+            regroup_weight(raw, cols)
+            quantise_weight(cols)
 
-        quantise_group(0, transpose_group(0))
+        grouped_of = {0: transpose_group(0), 1: transpose_group(1)}
+        for half in range(2):
+            quantise_half(0, half, grouped_of[0])
         nc.vector.tensor_scalar_mul(out=g_rows[0:1, 0, :], in0=g_rows[0:1, 0, :], scalar1=-1.0)
+
         for c in range(N_GROUPS):
-            more = c + 1 < N_GROUPS
-            if more:
-                grouped_next = transpose_group(c + 1)
-            for i in range(GROUP):
-                if more and i == GROUP // 2:
-                    quantise_group(c + 1, grouped_next)
-                j = c * GROUP + i
-                multiply_tile(j)
-                if (j + 1) % STORE_TILES == 0:
-                    store_tiles(slice(j + 1 - STORE_TILES, j + 1))
+            first = c * GROUP
+            for half in range(2):
+                if c + 1 < N_GROUPS:
+                    quantise_half(c + 1, half, grouped_of[c + 1])
+                for j in range(first + half * HALF, first + (half + 1) * HALF):
+                    multiply_by_a(j)
+                if half == 0:
+                    product_t = multiply_by_b(c)
+            if c + 2 < N_GROUPS:
+                grouped_of[c + 2] = transpose_group(c + 2)
+            transpose_back(c, product_t)
+            for half in range(2):
+                store_tiles(slice(first + half * HALF, first + (half + 1) * HALF))

from contextlib import ExitStack

import concourse.mybir as mybir
from concourse.masks import make_identity

BF16 = mybir.dt.bfloat16
F32 = mybir.dt.float32
U32 = mybir.dt.uint32
U8 = mybir.dt.uint8
E5M2_X4 = mybir.dt.float8_e5m2_x4
E4M3_X4 = mybir.dt.float8_e4m3fn_x4

P = 128
PACK = 4
NS = 512
NI = 128
NA = NS + NI
STEPS = 4096
TILES = STEPS // P
GROUP = 4
HALF = GROUP // 2
N_GROUPS = TILES // GROUP
WORDS = NS // 2

FLOPS = 2 * STEPS * NS * NA
BYTES = 2 * NS * NA + 2 * (STEPS + 1) * NS + 4 * (STEPS + 1) * NA


def tile_constrainnet_t_kernel(tc, A, B, x0, net_input, T, grad_out, out):
    nc = tc.nc
    assert T == STEPS + 1

    g_next = grad_out[NS : (STEPS + 1) * NS].rearrange("(p s k) -> p s k", p=P, k=NS)
    g_first = grad_out[0 : STEPS * NS].rearrange("(p s k) -> p s k", p=P, k=NS)[:, 0, :]
    g_last = grad_out[STEPS * NS : (STEPS + 1) * NS].rearrange("(o k) -> o k", o=1)
    d_rows = out[0 : STEPS * NA].rearrange("(p j n) -> p j n", p=P, n=NA)
    d_last = out[STEPS * NA : (STEPS + 1) * NA].rearrange("(o n) -> o n", o=1)

    with ExitStack() as ctx:
        ctx.enter_context(tc.manual_schedule())
        keep = ctx.enter_context(tc.tile_pool(name="keep", bufs=1))
        stage = ctx.enter_context(tc.tile_pool(name="stage", bufs=3))
        psum_t = ctx.enter_context(tc.psum_pool(name="psum_t", bufs=2))
        psum_a = ctx.enter_context(tc.psum_pool(name="psum_a", bufs=4))
        psum_b = ctx.enter_context(tc.psum_pool(name="psum_b", bufs=1))

        g_sb = keep.tile([P, (TILES + 1) * NS], BF16)
        g_rows = g_sb[:].rearrange("p (s k) -> p s k", k=NS)
        g_words = g_sb[:].bitcast(F32).rearrange("p (s w) -> p s w", w=WORDS)
        g_codes = keep.tile([P, TILES * P], U32, align_bytes=64)
        g_scales = keep.tile([P, TILES * P], U8, align_bytes=64)
        a_raw = keep.tile([P, PACK, NS], BF16)
        b_raw = keep.tile([P, PACK, NI], BF16)
        ab_grouped = keep.tile([P, NA, PACK], BF16, align_bytes=64)
        ab_codes = keep.tile([P, NA], U32, align_bytes=64)
        ab_scales = keep.tile([P, NA], U8, align_bytes=64)
        d_sb = keep.tile([P, TILES, NA], F32)
        g_last_sb = keep.tile([1, NS], BF16)
        d_last_sb = keep.tile([1, NA], F32)
        identity = keep.tile([P, P], F32)

        def load_weight(raw, weight):
            for u in range(2):
                nc.sync.dma_start(
                    out=raw[:, 2 * u : 2 * u + 2, :],
                    in_=weight[u * 2 * P : (u + 1) * 2 * P, :].rearrange("(q e) n -> q e n", e=2),
                )

        def load_group(c):
            nc.sync.dma_start(
                out=g_rows[:, 1 + c * GROUP : 1 + (c + 1) * GROUP, :],
                in_=g_next[:, c * GROUP : (c + 1) * GROUP, :],
            )

        def regroup_weight(raw, cols):
            nc.vector.tensor_copy(
                out=ab_grouped[:, cols, :].rearrange("p (c i) t -> p c t i", i=4),
                in_=raw[:].rearrange("p t (c i) -> p c t i", i=4),
            )

        def quantise_weight(cols):
            nc.vector.quantize_mx(
                out=ab_codes[:, cols].bitcast(E4M3_X4),
                scales=ab_scales[:, cols],
                in_=ab_grouped[:, cols, :].rearrange("p n t -> p (n t)"),
            )

        def transpose_group(c):
            grouped = stage.tile([P, GROUP * P * PACK], BF16, align_bytes=64)
            grouped_words = grouped[:].bitcast(F32).rearrange("p (j r u) -> p j r u", j=GROUP, u=2)
            for half in range(GROUP // 2):
                bank = psum_t.tile([P, 2, 2, P], F32)
                for i in range(2):
                    s = c * GROUP + 2 * half + i + 1
                    for u in range(2):
                        nc.tensor.transpose(
                            bank[:, i, u, :], g_words[:, s, u * P : (u + 1) * P], identity[:]
                        )
                nc.scalar.copy(
                    out=grouped_words[:, 2 * half : 2 * half + 2, :, :],
                    in_=bank[:].rearrange("p i u r -> p i r u"),
                )
            return grouped

        def quantise_half(c, half, grouped):
            first = 2 * half * P
            cols = slice(c * GROUP * P + first, c * GROUP * P + first + 2 * P)
            nc.vector.quantize_mx(
                out=g_codes[:, cols].bitcast(E5M2_X4),
                scales=g_scales[:, cols],
                in_=grouped[:, first * PACK : (first + 2 * P) * PACK],
            )

        def multiply_by_a(j):
            cols = slice(j * P, (j + 1) * P)
            acc = psum_a.tile([P, NS], F32)
            nc.tensor.matmul_mx(
                out=acc[:],
                lhsT=g_codes[:, cols].bitcast(E5M2_X4),
                lhsT_scale=g_scales[:, cols],
                rhs=ab_codes[:, 0:NS].bitcast(E4M3_X4),
                rhs_scale=ab_scales[:, 0:NS],
                start=True,
                stop=True,
            )
            nc.vector.tensor_tensor(
                out=d_sb[:, j, 0:NS], in0=acc[:], in1=g_rows[:, j, :], op=mybir.AluOpType.subtract
            )

        def multiply_by_b(c):
            cols = slice(c * GROUP * P, (c + 1) * GROUP * P)
            acc_t = psum_b.tile([P, GROUP * P], F32)
            nc.tensor.matmul_mx(
                out=acc_t[:],
                lhsT=ab_codes[:, NS:NA].bitcast(E4M3_X4),
                lhsT_scale=ab_scales[:, NS:NA],
                rhs=g_codes[:, cols].bitcast(E5M2_X4),
                rhs_scale=g_scales[:, cols],
                start=True,
                stop=True,
            )
            product_t = stage.tile([P, GROUP * P], F32)
            nc.scalar.copy(out=product_t[:], in_=acc_t[:])
            return product_t

        def transpose_back(c, product_t):
            bank = psum_b.tile([P, GROUP, P], F32)
            for i in range(GROUP):
                nc.tensor.transpose(bank[:, i, :], product_t[:, i * P : (i + 1) * P], identity[:])
            nc.scalar.copy(out=d_sb[:, c * GROUP : (c + 1) * GROUP, NS:NA], in_=bank[:])

        def store_tiles(tiles):
            nc.sync.dma_start(out=d_rows[:, tiles, :], in_=d_sb[:, tiles, :])

        nc.sync.dma_start(out=g_last_sb[:], in_=g_last)
        load_weight(a_raw, A)
        load_group(0)
        load_weight(b_raw, B)
        load_group(1)
        nc.sync.dma_start(out=g_rows[:, 0, :], in_=g_first)
        for c in range(2, N_GROUPS):
            load_group(c)

        make_identity(nc, identity[:])

        nc.vector.memset(d_last_sb[:, NS:NA], 0.0)
        nc.vector.tensor_scalar_mul(out=d_last_sb[:, 0:NS], in0=g_last_sb[:], scalar1=-1.0)
        nc.sync.dma_start(out=d_last, in_=d_last_sb[:])

        for raw, cols in ((a_raw, slice(0, NS)), (b_raw, slice(NS, NA))):
            regroup_weight(raw, cols)
            quantise_weight(cols)

        grouped_of = {0: transpose_group(0), 1: transpose_group(1)}
        for half in range(2):
            quantise_half(0, half, grouped_of[0])
        nc.vector.tensor_scalar_mul(out=g_rows[0:1, 0, :], in0=g_rows[0:1, 0, :], scalar1=-1.0)

        for c in range(N_GROUPS):
            first = c * GROUP
            for half in range(2):
                if c + 1 < N_GROUPS:
                    quantise_half(c + 1, half, grouped_of[c + 1])
                for j in range(first + half * HALF, first + (half + 1) * HALF):
                    multiply_by_a(j)
                if half == 0:
                    product_t = multiply_by_b(c)
            if c + 2 < N_GROUPS:
                grouped_of[c + 2] = transpose_group(c + 2)
            transpose_back(c, product_t)
            for half in range(2):
                store_tiles(slice(first + half * HALF, first + (half + 1) * HALF))
